import numpy as np
import ml_dtypes


def mxq(x, axis, fmt="e4m3"):
    dtype, down = {"e4m3": (ml_dtypes.float8_e4m3fn, 7), "e5m2": (ml_dtypes.float8_e5m2, 14)}[fmt]
    v = np.moveaxis(np.asarray(x, np.float32).astype(ml_dtypes.bfloat16).astype(np.float64), axis, -1)
    blocks = v.reshape(v.shape[:-1] + (-1, 32))
    amax = np.abs(blocks).max(-1, keepdims=True)
    byte = np.maximum(np.where(amax > 0, np.frexp(amax)[1] - 1 + 127, 0) - down, 1)
    scale = np.exp2(byte - 127.0)
    codes = (blocks / scale).astype(np.float32).astype(dtype).astype(np.float64)
    return np.moveaxis((codes * scale).reshape(v.shape), -1, axis)


WIDE = False


def mx_kscale(k):
    if not WIDE:
        return np.ones(k)
    levels = np.array([10, -10, 5, -5, 0])
    a = np.random.permutation(np.resize(levels, k // 512 * 4)).reshape(k // 512, 4)
    idx = np.arange(k)
    return np.exp2(a[idx // 512, idx % 128 // 32])


BF16 = ml_dtypes.bfloat16


def bf(x):
    return np.asarray(x, np.float32).astype(BF16)


def f64(x):
    return np.asarray(x).astype(np.float64)


B, D, E = 2, 1024, 256
S = E // 2


def rope(y):
    n = y.shape[-1]
    inv_freq = 1.0 / (10000.0 ** (np.arange(0.0, n, 2.0) / n))
    freqs = inv_freq * np.arange(y.shape[1], dtype=np.float64)
    sin = np.sin(freqs)[None, :, None]
    cos = np.cos(freqs)[None, :, None]
    y1 = y[..., ::2]
    y2 = y[..., 1::2]
    return np.concatenate([y1 * cos - y2 * sin, y1 * sin + y2 * cos], axis=-1)


def setup_inputs():
    s = mx_kscale(D)
    return {"x": bf(np.random.standard_normal((B, S, D)) * s),
            "Wk": bf(np.random.standard_normal((E, D)) / np.sqrt(D) / s[None, :]),
            "bk": bf(np.random.standard_normal(E) * 0.3),
            "Wq": bf(np.random.standard_normal((E, D)) / np.sqrt(D) / s[None, :]),
            "bq": bf(np.random.standard_normal(E) * 0.3),
            "Wv": bf(np.random.standard_normal((E, D)) / np.sqrt(D) / s[None, :]),
            "bv": bf(np.random.standard_normal(E) * 0.3)}


def reference(x, Wk, bk, Wq, bq, Wv, bv):
    xq = mxq(f64(x), 2, "e4m3")
    K = rope((xq @ mxq(f64(Wk), 1, "e4m3").T) + f64(bk))
    Q = rope((xq @ mxq(f64(Wq), 1, "e4m3").T) + f64(bq))
    V = (xq @ mxq(f64(Wv), 1, "e4m3").T) + f64(bv)
    return (K, Q, V)

@@ -1,0 +1,197 @@
+from contextlib import ExitStack
+
+import concourse.mybir as mybir
+from concourse.masks import make_identity
+
+F32 = mybir.dt.float32
+BF16 = mybir.dt.bfloat16
+U32 = mybir.dt.uint32
+U8 = mybir.dt.uint8
+FP8X4 = mybir.dt.float8_e4m3fn_x4
+ALU = mybir.AluOpType
+ACT = mybir.ActivationFunctionType
+
+P = 128
+B = 2
+D = 1024
+E = 256
+HALF = E // 2
+PASSES = D // (4 * P)
+WORDS = D // 2
+BANK = 512
+
+FLOPS = 2 * B * P * D * 3 * E
+
+
+def tile_attention_s_kernel(tc, x, Wk, bk, Wq, bq, Wv, bv, out_0, out_1, out_2):
+    nc = tc.nc
+    with ExitStack() as ctx:
+        consts = ctx.enter_context(tc.tile_pool(name="consts", bufs=1))
+        loads = ctx.enter_context(tc.tile_pool(name="loads", bufs=1))
+        stage = ctx.enter_context(tc.tile_pool(name="stage", bufs=3))
+        results = ctx.enter_context(tc.tile_pool(name="results", bufs=1))
+        psum_work = ctx.enter_context(tc.psum_pool(name="psum_work", bufs=5))
+        psum_acc = ctx.enter_context(tc.psum_pool(name="psum_acc", bufs=1))
+
+        bias_rows = consts.tile([P, 3 * E], BF16)
+        nc.vector.memset(bias_rows[:], 0.0)
+        for w, bias in enumerate((bk, bq, bv)):
+            nc.scalar.dma_start(
+                out=bias_rows[0:1, w * E : (w + 1) * E],
+                in_=bias.rearrange("(o e) -> o e", o=1),
+            )
+
+        even_odd = "(j e) d -> e j d"
+        sources = [
+            x[0],
+            x[1],
+            Wk.rearrange(even_odd, e=2)[0],
+            Wk.rearrange(even_odd, e=2)[1],
+            Wq.rearrange(even_odd, e=2)[0],
+            Wq.rearrange(even_odd, e=2)[1],
+            Wv[0:HALF, :],
+            Wv[HALF:E, :],
+        ]
+        raw = []
+        for i, source in enumerate(sources):
+            raw_i = loads.tile([P, D], BF16, name="raw%d" % i)
+            nc.sync.dma_start(out=raw_i[:], in_=source)
+            raw.append(raw_i)
+
+        ident = consts.tile([P, P], F32)
+        make_identity(nc, ident[:])
+        ones = consts.tile([P, P], BF16)
+        nc.vector.memset(ones[:], 1.0)
+
+        pos = consts.tile([P, 1], F32)
+        nc.gpsimd.iota(
+            pos[:], pattern=[[0, 1]], base=0, channel_multiplier=1,
+            allow_small_or_imprecise_dtypes=True,
+        )
+        exponent = consts.tile([P, 1], F32)
+        nc.gpsimd.tensor_scalar(
+            out=exponent[:], in0=pos[:], scalar1=-2.0 / E, scalar2=0.0, op0=ALU.mult, op1=ALU.add
+        )
+        ten_thousand = consts.tile([P, 1], F32)
+        nc.gpsimd.memset(ten_thousand[:], 10000.0)
+        theta = consts.tile([P, 1], F32)
+        nc.gpsimd.tensor_tensor(out=theta[:], in0=ten_thousand[:], in1=exponent[:], op=ALU.pow)
+        nc.gpsimd.tensor_tensor(out=theta[:], in0=theta[:], in1=pos[:], op=ALU.mult)
+        sines = consts.tile([P, 2], F32)
+        nc.scalar.activation(out=sines[:, 0:1], in_=theta[:], func=ACT.Sin, scale=0.5)
+        nc.scalar.activation(out=sines[:, 1:2], in_=theta[:], func=ACT.Sin, scale=0.25)
+        cosines = consts.tile([P, 2], F32)
+        nc.vector.scalar_tensor_tensor(
+            out=cosines[:], in0=sines[:], scalar=-2.0, in1=sines[:], op0=ALU.mult, op1=ALU.mult
+        )
+        nc.vector.tensor_scalar_add(out=cosines[:], in0=cosines[:], scalar1=1.0)
+        cos = cosines[:, 0:1]
+        plus_minus_sin = consts.tile([P, 2], F32)
+        for column, factor in enumerate((2.0, -2.0)):
+            nc.vector.scalar_tensor_tensor(
+                out=plus_minus_sin[:, column : column + 1],
+                in0=sines[:, 0:1], scalar=factor, in1=cosines[:, 1:2],
+                op0=ALU.mult, op1=ALU.mult,
+            )
+        sin = plus_minus_sin[:, 0:1]
+        neg_sin = plus_minus_sin[:, 1:2]
+
+        bias_kq = psum_work.tile([P, 2, HALF, 2], F32, tag="work")
+        nc.tensor.matmul(
+            out=bias_kq[:].rearrange("p w j e -> p (w j e)"),
+            lhsT=ones[:], rhs=bias_rows[:, 0 : 2 * E], start=True, stop=True,
+        )
+        bias_v_bank = psum_work.tile([P, E], F32, tag="work")
+        nc.tensor.matmul(
+            out=bias_v_bank[:], lhsT=ones[:], rhs=bias_rows[:, 2 * E : 3 * E], start=True, stop=True
+        )
+        bias_v = consts.tile([P, E], F32)
+        nc.scalar.copy(out=bias_v[:], in_=bias_v_bank[:])
+        bias_rot = consts.tile([P, 2, 2, HALF], F32)
+        bias_even = bias_kq[:, :, :, 0]
+        bias_odd = bias_kq[:, :, :, 1]
+        nc.scalar.activation(out=bias_rot[:, :, 0, :], in_=bias_odd, func=ACT.Copy, scale=neg_sin)
+        nc.scalar.activation(out=bias_rot[:, :, 1, :], in_=bias_even, func=ACT.Copy, scale=sin)
+        nc.vector.scalar_tensor_tensor(
+            out=bias_rot[:, :, 0, :], in0=bias_even, scalar=cos, in1=bias_rot[:, :, 0, :],
+            op0=ALU.mult, op1=ALU.add,
+        )
+        nc.vector.scalar_tensor_tensor(
+            out=bias_rot[:, :, 1, :], in0=bias_odd, scalar=cos, in1=bias_rot[:, :, 1, :],
+            op0=ALU.mult, op1=ALU.add,
+        )
+
+        codes = consts.tile([P, len(sources), PASSES, P], U32, align_bytes=64)
+        scales = consts.tile([P, len(sources), PASSES, P], U8, align_bytes=64)
+
+        def transpose_and_quantise(i):
+            words = raw[i][:].bitcast(F32)
+            turned = psum_work.tile([P, WORDS // P, P], F32, tag="work")
+            for c in range(WORDS // P):
+                nc.tensor.transpose(turned[:, c, :], words[:, c * P : (c + 1) * P], ident[:])
+            grouped = stage.tile([P, D], BF16, align_bytes=64)
+            nc.scalar.copy(
+                out=grouped[:].bitcast(F32).rearrange("q (g r u) -> q g r u", g=PASSES, u=2),
+                in_=turned[:].rearrange("q (g u) r -> q g r u", u=2),
+            )
+            nc.vector.quantize_mx(
+                out=codes[:, i].rearrange("q g r -> q (g r)").bitcast(FP8X4),
+                scales=scales[:, i].rearrange("q g r -> q (g r)"),
+                in_=grouped[:],
+            )
+
+        def project(acc, i, half):
+            for b in range(B):
+                for g in range(PASSES):
+                    nc.tensor.matmul_mx(
+                        out=acc[:, b, half, :],
+                        lhsT=codes[:, b, g, :].bitcast(FP8X4),
+                        lhsT_scale=scales[:, b, g, :],
+                        rhs=codes[:, i, g, :].bitcast(FP8X4),
+                        rhs_scale=scales[:, i, g, :],
+                        start=(g == 0),
+                        stop=(g == PASSES - 1),
+                    )
+
+        for b in range(B):
+            transpose_and_quantise(b)
+
+        for w, out_w in enumerate((out_0, out_1)):
+            acc = psum_acc.tile([P, B, 2, HALF], F32, name="acc%d" % w)
+            for half in range(2):
+                i = B + 2 * w + half
+                transpose_and_quantise(i)
+                project(acc, i, half)
+            rotated = results.tile([P, B, 2, HALF], F32, name="rotated%d" % w)
+            nc.vector.scalar_tensor_tensor(
+                out=rotated[:].rearrange("p b h j -> p b (h j)"),
+                in0=acc[:].rearrange("p b h j -> p b (h j)"),
+                scalar=cos,
+                in1=bias_rot[:, w].rearrange("p h j -> p (h j)").unsqueeze(1).to_broadcast([P, B, E]),
+                op0=ALU.mult, op1=ALU.add,
+            )
+            nc.vector.scalar_tensor_tensor(
+                out=rotated[:, :, 0, :], in0=acc[:, :, 1, :], scalar=neg_sin,
+                in1=rotated[:, :, 0, :], op0=ALU.mult, op1=ALU.add,
+            )
+            nc.vector.scalar_tensor_tensor(
+                out=rotated[:, :, 1, :], in0=acc[:, :, 0, :], scalar=sin,
+                in1=rotated[:, :, 1, :], op0=ALU.mult, op1=ALU.add,
+            )
+            nc.sync.dma_start(
+                out=out_w.rearrange("b s e -> s b e"),
+                in_=rotated[:].rearrange("p b h j -> p b (h j)"),
+            )
+
+        acc_v = psum_acc.tile([P, B, 2, HALF], F32)
+        for half in range(2):
+            i = B + 4 + half
+            transpose_and_quantise(i)
+            project(acc_v, i, half)
+            columns = slice(half * HALF, (half + 1) * HALF)
+            v_half = results.tile([P, B, HALF], F32, name="v_half%d" % half)
+            nc.vector.tensor_tensor(
+                out=v_half[:], in0=acc_v[:, :, half, :],
+                in1=bias_v[:, columns].unsqueeze(1).to_broadcast([P, B, HALF]), op=ALU.add,
+            )
+            nc.sync.dma_start(out=out_2.rearrange("b s e -> s b e")[:, :, columns], in_=v_half[:])

@@ -26,6 +26,7 @@ FLOPS = 2 * B * P * D * 3 * E
 def tile_attention_s_kernel(tc, x, Wk, bk, Wq, bq, Wv, bv, out_0, out_1, out_2):
     nc = tc.nc
     with ExitStack() as ctx:
+        ctx.enter_context(tc.manual_schedule())
         consts = ctx.enter_context(tc.tile_pool(name="consts", bufs=1))
         loads = ctx.enter_context(tc.tile_pool(name="loads", bufs=1))
         stage = ctx.enter_context(tc.tile_pool(name="stage", bufs=3))
@@ -58,8 +59,6 @@ def tile_attention_s_kernel(tc, x, Wk, bk, Wq, bq, Wv, bv, out_0, out_1, out_2):
             nc.sync.dma_start(out=raw_i[:], in_=source)
             raw.append(raw_i)
 
-        ident = consts.tile([P, P], F32)
-        make_identity(nc, ident[:])
         ones = consts.tile([P, P], BF16)
         nc.vector.memset(ones[:], 1.0)
 
@@ -77,6 +76,8 @@ def tile_attention_s_kernel(tc, x, Wk, bk, Wq, bq, Wv, bv, out_0, out_1, out_2):
         theta = consts.tile([P, 1], F32)
         nc.gpsimd.tensor_tensor(out=theta[:], in0=ten_thousand[:], in1=exponent[:], op=ALU.pow)
         nc.gpsimd.tensor_tensor(out=theta[:], in0=theta[:], in1=pos[:], op=ALU.mult)
+        ident = consts.tile([P, P], F32)
+        make_identity(nc, ident[:])
         sines = consts.tile([P, 2], F32)
         nc.scalar.activation(out=sines[:, 0:1], in_=theta[:], func=ACT.Sin, scale=0.5)
         nc.scalar.activation(out=sines[:, 1:2], in_=theta[:], func=ACT.Sin, scale=0.25)
@@ -153,15 +154,7 @@ def tile_attention_s_kernel(tc, x, Wk, bk, Wq, bq, Wv, bv, out_0, out_1, out_2):
                         stop=(g == PASSES - 1),
                     )
 
-        for b in range(B):
-            transpose_and_quantise(b)
-
-        for w, out_w in enumerate((out_0, out_1)):
-            acc = psum_acc.tile([P, B, 2, HALF], F32, name="acc%d" % w)
-            for half in range(2):
-                i = B + 2 * w + half
-                transpose_and_quantise(i)
-                project(acc, i, half)
+        def rotate_and_store(acc, w, out_w):
             rotated = results.tile([P, B, 2, HALF], F32, name="rotated%d" % w)
             nc.vector.scalar_tensor_tensor(
                 out=rotated[:].rearrange("p b h j -> p b (h j)"),
@@ -183,15 +176,33 @@ def tile_attention_s_kernel(tc, x, Wk, bk, Wq, bq, Wv, bv, out_0, out_1, out_2):
                 in_=rotated[:].rearrange("p b h j -> p b (h j)"),
             )
 
-        acc_v = psum_acc.tile([P, B, 2, HALF], F32)
-        for half in range(2):
-            i = B + 4 + half
-            transpose_and_quantise(i)
-            project(acc_v, i, half)
+        def add_bias_and_store(acc, half):
             columns = slice(half * HALF, (half + 1) * HALF)
             v_half = results.tile([P, B, HALF], F32, name="v_half%d" % half)
             nc.vector.tensor_tensor(
-                out=v_half[:], in0=acc_v[:, :, half, :],
+                out=v_half[:], in0=acc[:, :, half, :],
                 in1=bias_v[:, columns].unsqueeze(1).to_broadcast([P, B, HALF]), op=ALU.add,
             )
             nc.sync.dma_start(out=out_2.rearrange("b s e -> s b e")[:, :, columns], in_=v_half[:])
+
+        def tiles_of(w):
+            return (B + 2 * w, B + 2 * w + 1)
+
+        for i in range(B):
+            transpose_and_quantise(i)
+        for i in tiles_of(0):
+            transpose_and_quantise(i)
+        for w in range(3):
+            if w + 1 < 3:
+                for i in tiles_of(w + 1):
+                    transpose_and_quantise(i)
+            acc = psum_acc.tile([P, B, 2, HALF], F32, name="acc%d" % w)
+            for half, i in enumerate(tiles_of(w)):
+                project(acc, i, half)
+            if w == 0:
+                rotate_and_store(acc, w, out_0)
+            elif w == 1:
+                rotate_and_store(acc, w, out_1)
+            else:
+                for half in range(2):
+                    add_bias_and_store(acc, half)

@@ -19,6 +19,8 @@ HALF = E // 2
 PASSES = D // (4 * P)
 WORDS = D // 2
 BANK = 512
+WARM_COLUMNS = 256
+WARM_PASSES = 24
 
 FLOPS = 2 * B * P * D * 3 * E
 
@@ -40,6 +42,23 @@ def tile_attention_s_kernel(tc, x, Wk, bk, Wq, bq, Wv, bv, out_0, out_1, out_2):
             nc.scalar.dma_start(
                 out=bias_rows[0:1, w * E : (w + 1) * E],
                 in_=bias.rearrange("(o e) -> o e", o=1),
+            )
+
+        zeros = consts.tile([P, 4 * WARM_COLUMNS], BF16, align_bytes=64)
+        zero_codes = consts.tile([P, WARM_COLUMNS], U32, align_bytes=64)
+        zero_scales = consts.tile([P, WARM_COLUMNS], U8, align_bytes=64)
+        nc.vector.memset(zeros[:], 0.0)
+        nc.vector.quantize_mx(out=zero_codes[:].bitcast(FP8X4), scales=zero_scales[:], in_=zeros[:])
+        unread = psum_work.tile([P, WARM_COLUMNS], F32, tag="work")
+        for n in range(WARM_PASSES):
+            nc.tensor.matmul_mx(
+                out=unread[:],
+                lhsT=zero_codes[:, 0:P].bitcast(FP8X4),
+                lhsT_scale=zero_scales[:, 0:P],
+                rhs=zero_codes[:].bitcast(FP8X4),
+                rhs_scale=zero_scales[:],
+                start=True,
+                stop=True,
             )
 
         even_odd = "(j e) d -> e j d"

@@ -18,9 +18,11 @@ E = 256
 HALF = E // 2
 PASSES = D // (4 * P)
 WORDS = D // 2
-BANK = 512
-WARM_COLUMNS = 256
-WARM_PASSES = 24
+
+X_TILES = (0, 1)
+K_TILES = (2, 3)
+Q_TILES = (4, 5)
+V_TILES = (6, 7)
 
 FLOPS = 2 * B * P * D * 3 * E
 
@@ -34,33 +36,10 @@ def tile_attention_s_kernel(tc, x, Wk, bk, Wq, bq, Wv, bv, out_0, out_1, out_2):
         stage = ctx.enter_context(tc.tile_pool(name="stage", bufs=3))
         results = ctx.enter_context(tc.tile_pool(name="results", bufs=1))
         psum_work = ctx.enter_context(tc.psum_pool(name="psum_work", bufs=5))
-        psum_acc = ctx.enter_context(tc.psum_pool(name="psum_acc", bufs=1))
+        psum_acc = ctx.enter_context(tc.psum_pool(name="psum_acc", bufs=3))
 
         bias_rows = consts.tile([P, 3 * E], BF16)
         nc.vector.memset(bias_rows[:], 0.0)
-        for w, bias in enumerate((bk, bq, bv)):
-            nc.scalar.dma_start(
-                out=bias_rows[0:1, w * E : (w + 1) * E],
-                in_=bias.rearrange("(o e) -> o e", o=1),
-            )
-
-        zeros = consts.tile([P, 4 * WARM_COLUMNS], BF16, align_bytes=64)
-        zero_codes = consts.tile([P, WARM_COLUMNS], U32, align_bytes=64)
-        zero_scales = consts.tile([P, WARM_COLUMNS], U8, align_bytes=64)
-        nc.vector.memset(zeros[:], 0.0)
-        nc.vector.quantize_mx(out=zero_codes[:].bitcast(FP8X4), scales=zero_scales[:], in_=zeros[:])
-        unread = psum_work.tile([P, WARM_COLUMNS], F32, tag="work")
-        for n in range(WARM_PASSES):
-            nc.tensor.matmul_mx(
-                out=unread[:],
-                lhsT=zero_codes[:, 0:P].bitcast(FP8X4),
-                lhsT_scale=zero_scales[:, 0:P],
-                rhs=zero_codes[:].bitcast(FP8X4),
-                rhs_scale=zero_scales[:],
-                start=True,
-                stop=True,
-            )
-
         even_odd = "(j e) d -> e j d"
         sources = [
             x[0],
@@ -77,7 +56,15 @@ def tile_attention_s_kernel(tc, x, Wk, bk, Wq, bq, Wv, bv, out_0, out_1, out_2):
             raw_i = loads.tile([P, D], BF16, name="raw%d" % i)
             nc.sync.dma_start(out=raw_i[:], in_=source)
             raw.append(raw_i)
+            if i == X_TILES[-1]:
+                for w, bias in enumerate((bk, bq, bv)):
+                    nc.sync.dma_start(
+                        out=bias_rows[0:1, w * E : (w + 1) * E],
+                        in_=bias.rearrange("(o e) -> o e", o=1),
+                    )
 
+        ident = consts.tile([P, P], F32)
+        make_identity(nc, ident[:])
         ones = consts.tile([P, P], BF16)
         nc.vector.memset(ones[:], 1.0)
 
@@ -95,11 +82,74 @@ def tile_attention_s_kernel(tc, x, Wk, bk, Wq, bq, Wv, bv, out_0, out_1, out_2):
         theta = consts.tile([P, 1], F32)
         nc.gpsimd.tensor_tensor(out=theta[:], in0=ten_thousand[:], in1=exponent[:], op=ALU.pow)
         nc.gpsimd.tensor_tensor(out=theta[:], in0=theta[:], in1=pos[:], op=ALU.mult)
-        ident = consts.tile([P, P], F32)
-        make_identity(nc, ident[:])
         sines = consts.tile([P, 2], F32)
         nc.scalar.activation(out=sines[:, 0:1], in_=theta[:], func=ACT.Sin, scale=0.5)
         nc.scalar.activation(out=sines[:, 1:2], in_=theta[:], func=ACT.Sin, scale=0.25)
+
+        codes = consts.tile([P, len(sources), PASSES, P], U32, align_bytes=64)
+        scales = consts.tile([P, len(sources), PASSES, P], U8, align_bytes=64)
+
+        def transpose(i, copy_out):
+            words = raw[i][:].bitcast(F32)
+            turned = psum_work.tile([P, WORDS // P, P], F32, tag="work")
+            for c in range(WORDS // P):
+                nc.tensor.transpose(turned[:, c, :], words[:, c * P : (c + 1) * P], ident[:])
+            grouped = stage.tile([P, D], BF16, align_bytes=64)
+            copy_out(
+                out=grouped[:].bitcast(F32).rearrange("q (g r u) -> q g r u", g=PASSES, u=2),
+                in_=turned[:].rearrange("q (g u) r -> q g r u", u=2),
+            )
+            return grouped
+
+        def quantise(i, grouped):
+            nc.vector.quantize_mx(
+                out=codes[:, i].rearrange("q g r -> q (g r)").bitcast(FP8X4),
+                scales=scales[:, i].rearrange("q g r -> q (g r)"),
+                in_=grouped[:],
+            )
+
+        def project(acc_columns, i):
+            for b in X_TILES:
+                for g in range(PASSES):
+                    nc.tensor.matmul_mx(
+                        out=acc_columns[:, b, :],
+                        lhsT=codes[:, b, g, :].bitcast(FP8X4),
+                        lhsT_scale=scales[:, b, g, :],
+                        rhs=codes[:, i, g, :].bitcast(FP8X4),
+                        rhs_scale=scales[:, i, g, :],
+                        start=(g == 0),
+                        stop=(g == PASSES - 1),
+                    )
+
+        def project_rotate_store(tiles, bias_rot_w, out_w):
+            acc = psum_acc.tile([P, B, 2, HALF], F32, tag="acc")
+            for half, i in enumerate(tiles):
+                project(acc[:, :, half, :], i)
+            rotated = results.tile([P, B, 2, HALF], F32, name="rotated%d" % tiles[0])
+            nc.vector.scalar_tensor_tensor(
+                out=rotated[:].rearrange("p b h j -> p b (h j)"),
+                in0=acc[:].rearrange("p b h j -> p b (h j)"),
+                scalar=cos,
+                in1=bias_rot_w.rearrange("p h j -> p (h j)").unsqueeze(1).to_broadcast([P, B, E]),
+                op0=ALU.mult, op1=ALU.add,
+            )
+            nc.vector.scalar_tensor_tensor(
+                out=rotated[:, :, 0, :], in0=acc[:, :, 1, :], scalar=neg_sin,
+                in1=rotated[:, :, 0, :], op0=ALU.mult, op1=ALU.add,
+            )
+            nc.vector.scalar_tensor_tensor(
+                out=rotated[:, :, 1, :], in0=acc[:, :, 0, :], scalar=sin,
+                in1=rotated[:, :, 1, :], op0=ALU.mult, op1=ALU.add,
+            )
+            nc.sync.dma_start(
+                out=out_w.rearrange("b s e -> s b e"),
+                in_=rotated[:].rearrange("p b h j -> p b (h j)"),
+            )
+
+        grouped_x = [transpose(i, nc.vector.tensor_copy) for i in X_TILES]
+        for i in X_TILES:
+            quantise(i, grouped_x[i])
+
         cosines = consts.tile([P, 2], F32)
         nc.vector.scalar_tensor_tensor(
             out=cosines[:], in0=sines[:], scalar=-2.0, in1=sines[:], op0=ALU.mult, op1=ALU.mult
@@ -116,6 +166,9 @@ def tile_attention_s_kernel(tc, x, Wk, bk, Wq, bq, Wv, bv, out_0, out_1, out_2):
         sin = plus_minus_sin[:, 0:1]
         neg_sin = plus_minus_sin[:, 1:2]
 
+        for i in K_TILES:
+            quantise(i, transpose(i, nc.scalar.copy))
+
         bias_kq = psum_work.tile([P, 2, HALF, 2], F32, tag="work")
         nc.tensor.matmul(
             out=bias_kq[:].rearrange("p w j e -> p (w j e)"),
@@ -125,8 +178,6 @@ def tile_attention_s_kernel(tc, x, Wk, bk, Wq, bq, Wv, bv, out_0, out_1, out_2):
         nc.tensor.matmul(
             out=bias_v_bank[:], lhsT=ones[:], rhs=bias_rows[:, 2 * E : 3 * E], start=True, stop=True
         )
-        bias_v = consts.tile([P, E], F32)
-        nc.scalar.copy(out=bias_v[:], in_=bias_v_bank[:])
         bias_rot = consts.tile([P, 2, 2, HALF], F32)
         bias_even = bias_kq[:, :, :, 0]
         bias_odd = bias_kq[:, :, :, 1]
@@ -141,87 +192,23 @@ def tile_attention_s_kernel(tc, x, Wk, bk, Wq, bq, Wv, bv, out_0, out_1, out_2):
             op0=ALU.mult, op1=ALU.add,
         )
 
-        codes = consts.tile([P, len(sources), PASSES, P], U32, align_bytes=64)
-        scales = consts.tile([P, len(sources), PASSES, P], U8, align_bytes=64)
+        for i in Q_TILES:
+            quantise(i, transpose(i, nc.scalar.copy))
+        project_rotate_store(K_TILES, bias_rot[:, 0], out_0)
 
-        def transpose_and_quantise(i):
-            words = raw[i][:].bitcast(F32)
-            turned = psum_work.tile([P, WORDS // P, P], F32, tag="work")
-            for c in range(WORDS // P):
-                nc.tensor.transpose(turned[:, c, :], words[:, c * P : (c + 1) * P], ident[:])
-            grouped = stage.tile([P, D], BF16, align_bytes=64)
-            nc.scalar.copy(
-                out=grouped[:].bitcast(F32).rearrange("q (g r u) -> q g r u", g=PASSES, u=2),
-                in_=turned[:].rearrange("q (g u) r -> q g r u", u=2),
-            )
-            nc.vector.quantize_mx(
-                out=codes[:, i].rearrange("q g r -> q (g r)").bitcast(FP8X4),
-                scales=scales[:, i].rearrange("q g r -> q (g r)"),
-                in_=grouped[:],
-            )
+        bias_v = consts.tile([P, E], F32)
+        nc.scalar.copy(out=bias_v[:], in_=bias_v_bank[:])
+        for i in V_TILES:
+            quantise(i, transpose(i, nc.scalar.copy))
+        project_rotate_store(Q_TILES, bias_rot[:, 1], out_1)
 
-        def project(acc, i, half):
-            for b in range(B):
-                for g in range(PASSES):
-                    nc.tensor.matmul_mx(
-                        out=acc[:, b, half, :],
-                        lhsT=codes[:, b, g, :].bitcast(FP8X4),
-                        lhsT_scale=scales[:, b, g, :],
-                        rhs=codes[:, i, g, :].bitcast(FP8X4),
-                        rhs_scale=scales[:, i, g, :],
-                        start=(g == 0),
-                        stop=(g == PASSES - 1),
-                    )
-
-        def rotate_and_store(acc, w, out_w):
-            rotated = results.tile([P, B, 2, HALF], F32, name="rotated%d" % w)
-            nc.vector.scalar_tensor_tensor(
-                out=rotated[:].rearrange("p b h j -> p b (h j)"),
-                in0=acc[:].rearrange("p b h j -> p b (h j)"),
-                scalar=cos,
-                in1=bias_rot[:, w].rearrange("p h j -> p (h j)").unsqueeze(1).to_broadcast([P, B, E]),
-                op0=ALU.mult, op1=ALU.add,
-            )
-            nc.vector.scalar_tensor_tensor(
-                out=rotated[:, :, 0, :], in0=acc[:, :, 1, :], scalar=neg_sin,
-                in1=rotated[:, :, 0, :], op0=ALU.mult, op1=ALU.add,
-            )
-            nc.vector.scalar_tensor_tensor(
-                out=rotated[:, :, 1, :], in0=acc[:, :, 0, :], scalar=sin,
-                in1=rotated[:, :, 1, :], op0=ALU.mult, op1=ALU.add,
-            )
-            nc.sync.dma_start(
-                out=out_w.rearrange("b s e -> s b e"),
-                in_=rotated[:].rearrange("p b h j -> p b (h j)"),
-            )
-
-        def add_bias_and_store(acc, half):
+        for half, i in enumerate(V_TILES):
             columns = slice(half * HALF, (half + 1) * HALF)
+            acc_v = psum_acc.tile([P, B, HALF], F32, tag="acc")
+            project(acc_v, i)
             v_half = results.tile([P, B, HALF], F32, name="v_half%d" % half)
             nc.vector.tensor_tensor(
-                out=v_half[:], in0=acc[:, :, half, :],
+                out=v_half[:], in0=acc_v[:],
                 in1=bias_v[:, columns].unsqueeze(1).to_broadcast([P, B, HALF]), op=ALU.add,
             )
             nc.sync.dma_start(out=out_2.rearrange("b s e -> s b e")[:, :, columns], in_=v_half[:])
-
-        def tiles_of(w):
-            return (B + 2 * w, B + 2 * w + 1)
-
-        for i in range(B):
-            transpose_and_quantise(i)
-        for i in tiles_of(0):
-            transpose_and_quantise(i)
-        for w in range(3):
-            if w + 1 < 3:
-                for i in tiles_of(w + 1):
-                    transpose_and_quantise(i)
-            acc = psum_acc.tile([P, B, 2, HALF], F32, name="acc%d" % w)
-            for half, i in enumerate(tiles_of(w)):
-                project(acc, i, half)
-            if w == 0:
-                rotate_and_store(acc, w, out_0)
-            elif w == 1:
-                rotate_and_store(acc, w, out_1)
-            else:
-                for half in range(2):
-                    add_bias_and_store(acc, half)

@@ -30,7 +30,6 @@ FLOPS = 2 * B * P * D * 3 * E
 def tile_attention_s_kernel(tc, x, Wk, bk, Wq, bq, Wv, bv, out_0, out_1, out_2):
     nc = tc.nc
     with ExitStack() as ctx:
-        ctx.enter_context(tc.manual_schedule())
         consts = ctx.enter_context(tc.tile_pool(name="consts", bufs=1))
         loads = ctx.enter_context(tc.tile_pool(name="loads", bufs=1))
         stage = ctx.enter_context(tc.tile_pool(name="stage", bufs=3))

@@ -145,7 +145,7 @@ def tile_attention_s_kernel(tc, x, Wk, bk, Wq, bq, Wv, bv, out_0, out_1, out_2):
                 in_=rotated[:].rearrange("p b h j -> p b (h j)"),
             )
 
-        grouped_x = [transpose(i, nc.vector.tensor_copy) for i in X_TILES]
+        grouped_x = [transpose(i, nc.scalar.copy) for i in X_TILES]
         for i in X_TILES:
             quantise(i, grouped_x[i])
 

@@ -55,7 +55,7 @@ def tile_attention_s_kernel(tc, x, Wk, bk, Wq, bq, Wv, bv, out_0, out_1, out_2):
             raw_i = loads.tile([P, D], BF16, name="raw%d" % i)
             nc.sync.dma_start(out=raw_i[:], in_=source)
             raw.append(raw_i)
-            if i == X_TILES[-1]:
+            if i == K_TILES[-1]:
                 for w, bias in enumerate((bk, bq, bv)):
                     nc.sync.dma_start(
                         out=bias_rows[0:1, w * E : (w + 1) * E],

from contextlib import ExitStack

import concourse.mybir as mybir
from concourse.masks import make_identity

F32 = mybir.dt.float32
BF16 = mybir.dt.bfloat16
U32 = mybir.dt.uint32
U8 = mybir.dt.uint8
FP8X4 = mybir.dt.float8_e4m3fn_x4
ALU = mybir.AluOpType
ACT = mybir.ActivationFunctionType

P = 128
B = 2
D = 1024
E = 256
HALF = E // 2
PASSES = D // (4 * P)
WORDS = D // 2

X_TILES = (0, 1)
K_TILES = (2, 3)
Q_TILES = (4, 5)
V_TILES = (6, 7)

FLOPS = 2 * B * P * D * 3 * E


def tile_attention_s_kernel(tc, x, Wk, bk, Wq, bq, Wv, bv, out_0, out_1, out_2):
    nc = tc.nc
    with ExitStack() as ctx:
        consts = ctx.enter_context(tc.tile_pool(name="consts", bufs=1))
        loads = ctx.enter_context(tc.tile_pool(name="loads", bufs=1))
        stage = ctx.enter_context(tc.tile_pool(name="stage", bufs=3))
        results = ctx.enter_context(tc.tile_pool(name="results", bufs=1))
        psum_work = ctx.enter_context(tc.psum_pool(name="psum_work", bufs=5))
        psum_acc = ctx.enter_context(tc.psum_pool(name="psum_acc", bufs=3))

        bias_rows = consts.tile([P, 3 * E], BF16)
        nc.vector.memset(bias_rows[:], 0.0)
        even_odd = "(j e) d -> e j d"
        sources = [
            x[0],
            x[1],
            Wk.rearrange(even_odd, e=2)[0],
            Wk.rearrange(even_odd, e=2)[1],
            Wq.rearrange(even_odd, e=2)[0],
            Wq.rearrange(even_odd, e=2)[1],
            Wv[0:HALF, :],
            Wv[HALF:E, :],
        ]
        raw = []
        for i, source in enumerate(sources):
            raw_i = loads.tile([P, D], BF16, name="raw%d" % i)
            nc.sync.dma_start(out=raw_i[:], in_=source)
            raw.append(raw_i)
            if i == K_TILES[-1]:
                for w, bias in enumerate((bk, bq, bv)):
                    nc.sync.dma_start(
                        out=bias_rows[0:1, w * E : (w + 1) * E],
                        in_=bias.rearrange("(o e) -> o e", o=1),
                    )

        ident = consts.tile([P, P], F32)
        make_identity(nc, ident[:])
        ones = consts.tile([P, P], BF16)
        nc.vector.memset(ones[:], 1.0)

        pos = consts.tile([P, 1], F32)
        nc.gpsimd.iota(
            pos[:], pattern=[[0, 1]], base=0, channel_multiplier=1,
            allow_small_or_imprecise_dtypes=True,
        )
        exponent = consts.tile([P, 1], F32)
        nc.gpsimd.tensor_scalar(
            out=exponent[:], in0=pos[:], scalar1=-2.0 / E, scalar2=0.0, op0=ALU.mult, op1=ALU.add
        )
        ten_thousand = consts.tile([P, 1], F32)
        nc.gpsimd.memset(ten_thousand[:], 10000.0)
        theta = consts.tile([P, 1], F32)
        nc.gpsimd.tensor_tensor(out=theta[:], in0=ten_thousand[:], in1=exponent[:], op=ALU.pow)
        nc.gpsimd.tensor_tensor(out=theta[:], in0=theta[:], in1=pos[:], op=ALU.mult)
        sines = consts.tile([P, 2], F32)
        nc.scalar.activation(out=sines[:, 0:1], in_=theta[:], func=ACT.Sin, scale=0.5)
        nc.scalar.activation(out=sines[:, 1:2], in_=theta[:], func=ACT.Sin, scale=0.25)

        codes = consts.tile([P, len(sources), PASSES, P], U32, align_bytes=64)
        scales = consts.tile([P, len(sources), PASSES, P], U8, align_bytes=64)

        def transpose(i, copy_out):
            words = raw[i][:].bitcast(F32)
            turned = psum_work.tile([P, WORDS // P, P], F32, tag="work")
            for c in range(WORDS // P):
                nc.tensor.transpose(turned[:, c, :], words[:, c * P : (c + 1) * P], ident[:])
            grouped = stage.tile([P, D], BF16, align_bytes=64)
            copy_out(
                out=grouped[:].bitcast(F32).rearrange("q (g r u) -> q g r u", g=PASSES, u=2),
                in_=turned[:].rearrange("q (g u) r -> q g r u", u=2),
            )
            return grouped

        def quantise(i, grouped):
            nc.vector.quantize_mx(
                out=codes[:, i].rearrange("q g r -> q (g r)").bitcast(FP8X4),
                scales=scales[:, i].rearrange("q g r -> q (g r)"),
                in_=grouped[:],
            )

        def project(acc_columns, i):
            for b in X_TILES:
                for g in range(PASSES):
                    nc.tensor.matmul_mx(
                        out=acc_columns[:, b, :],
                        lhsT=codes[:, b, g, :].bitcast(FP8X4),
                        lhsT_scale=scales[:, b, g, :],
                        rhs=codes[:, i, g, :].bitcast(FP8X4),
                        rhs_scale=scales[:, i, g, :],
                        start=(g == 0),
                        stop=(g == PASSES - 1),
                    )

        def project_rotate_store(tiles, bias_rot_w, out_w):
            acc = psum_acc.tile([P, B, 2, HALF], F32, tag="acc")
            for half, i in enumerate(tiles):
                project(acc[:, :, half, :], i)
            rotated = results.tile([P, B, 2, HALF], F32, name="rotated%d" % tiles[0])
            nc.vector.scalar_tensor_tensor(
                out=rotated[:].rearrange("p b h j -> p b (h j)"),
                in0=acc[:].rearrange("p b h j -> p b (h j)"),
                scalar=cos,
                in1=bias_rot_w.rearrange("p h j -> p (h j)").unsqueeze(1).to_broadcast([P, B, E]),
                op0=ALU.mult, op1=ALU.add,
            )
            nc.vector.scalar_tensor_tensor(
                out=rotated[:, :, 0, :], in0=acc[:, :, 1, :], scalar=neg_sin,
                in1=rotated[:, :, 0, :], op0=ALU.mult, op1=ALU.add,
            )
            nc.vector.scalar_tensor_tensor(
                out=rotated[:, :, 1, :], in0=acc[:, :, 0, :], scalar=sin,
                in1=rotated[:, :, 1, :], op0=ALU.mult, op1=ALU.add,
            )
            nc.sync.dma_start(
                out=out_w.rearrange("b s e -> s b e"),
                in_=rotated[:].rearrange("p b h j -> p b (h j)"),
            )

        grouped_x = [transpose(i, nc.scalar.copy) for i in X_TILES]
        for i in X_TILES:
            quantise(i, grouped_x[i])

        cosines = consts.tile([P, 2], F32)
        nc.vector.scalar_tensor_tensor(
            out=cosines[:], in0=sines[:], scalar=-2.0, in1=sines[:], op0=ALU.mult, op1=ALU.mult
        )
        nc.vector.tensor_scalar_add(out=cosines[:], in0=cosines[:], scalar1=1.0)
        cos = cosines[:, 0:1]
        plus_minus_sin = consts.tile([P, 2], F32)
        for column, factor in enumerate((2.0, -2.0)):
            nc.vector.scalar_tensor_tensor(
                out=plus_minus_sin[:, column : column + 1],
                in0=sines[:, 0:1], scalar=factor, in1=cosines[:, 1:2],
                op0=ALU.mult, op1=ALU.mult,
            )
        sin = plus_minus_sin[:, 0:1]
        neg_sin = plus_minus_sin[:, 1:2]

        for i in K_TILES:
            quantise(i, transpose(i, nc.scalar.copy))

        bias_kq = psum_work.tile([P, 2, HALF, 2], F32, tag="work")
        nc.tensor.matmul(
            out=bias_kq[:].rearrange("p w j e -> p (w j e)"),
            lhsT=ones[:], rhs=bias_rows[:, 0 : 2 * E], start=True, stop=True,
        )
        bias_v_bank = psum_work.tile([P, E], F32, tag="work")
        nc.tensor.matmul(
            out=bias_v_bank[:], lhsT=ones[:], rhs=bias_rows[:, 2 * E : 3 * E], start=True, stop=True
        )
        bias_rot = consts.tile([P, 2, 2, HALF], F32)
        bias_even = bias_kq[:, :, :, 0]
        bias_odd = bias_kq[:, :, :, 1]
        nc.scalar.activation(out=bias_rot[:, :, 0, :], in_=bias_odd, func=ACT.Copy, scale=neg_sin)
        nc.scalar.activation(out=bias_rot[:, :, 1, :], in_=bias_even, func=ACT.Copy, scale=sin)
        nc.vector.scalar_tensor_tensor(
            out=bias_rot[:, :, 0, :], in0=bias_even, scalar=cos, in1=bias_rot[:, :, 0, :],
            op0=ALU.mult, op1=ALU.add,
        )
        nc.vector.scalar_tensor_tensor(
            out=bias_rot[:, :, 1, :], in0=bias_odd, scalar=cos, in1=bias_rot[:, :, 1, :],
            op0=ALU.mult, op1=ALU.add,
        )

        for i in Q_TILES:
            quantise(i, transpose(i, nc.scalar.copy))
        project_rotate_store(K_TILES, bias_rot[:, 0], out_0)

        bias_v = consts.tile([P, E], F32)
        nc.scalar.copy(out=bias_v[:], in_=bias_v_bank[:])
        for i in V_TILES:
            quantise(i, transpose(i, nc.scalar.copy))
        project_rotate_store(Q_TILES, bias_rot[:, 1], out_1)

        for half, i in enumerate(V_TILES):
            columns = slice(half * HALF, (half + 1) * HALF)
            acc_v = psum_acc.tile([P, B, HALF], F32, tag="acc")
            project(acc_v, i)
            v_half = results.tile([P, B, HALF], F32, name="v_half%d" % half)
            nc.vector.tensor_tensor(
                out=v_half[:], in0=acc_v[:],
                in1=bias_v[:, columns].unsqueeze(1).to_broadcast([P, B, HALF]), op=ALU.add,
            )
            nc.sync.dma_start(out=out_2.rearrange("b s e -> s b e")[:, :, columns], in_=v_half[:])
